import numpy as np
import ml_dtypes


def mxq(x, axis, fmt="e4m3"):
    dtype, down = {"e4m3": (ml_dtypes.float8_e4m3fn, 7), "e5m2": (ml_dtypes.float8_e5m2, 14)}[fmt]
    v = np.moveaxis(np.asarray(x, np.float32).astype(ml_dtypes.bfloat16).astype(np.float64), axis, -1)
    blocks = v.reshape(v.shape[:-1] + (-1, 32))
    amax = np.abs(blocks).max(-1, keepdims=True)
    byte = np.maximum(np.where(amax > 0, np.frexp(amax)[1] - 1 + 127, 0) - down, 1)
    scale = np.exp2(byte - 127.0)
    codes = (blocks / scale).astype(np.float32).astype(dtype).astype(np.float64)
    return np.moveaxis((codes * scale).reshape(v.shape), -1, axis)


WIDE = False


def mx_kscale(k):
    if not WIDE:
        return np.ones(k)
    levels = np.array([10, -10, 5, -5, 0])
    a = np.random.permutation(np.resize(levels, k // 512 * 4)).reshape(k // 512, 4)
    idx = np.arange(k)
    return np.exp2(a[idx // 512, idx % 128 // 32])


BF16 = ml_dtypes.bfloat16


def bf(x):
    return np.asarray(x, np.float32).astype(BF16)


def f64(x):
    return np.asarray(x).astype(np.float64)


E2M1 = np.array([0.0, 0.5, 1.0, 1.5, 2.0, 3.0, 4.0, 6.0, -0.0, -0.5, -1.0, -1.5, -2.0, -3.0, -4.0, -6.0])


def pack_weight(w, fmt):
    k, n = w.shape
    w = f64(bf(w)).reshape(k // 32, 32, n)
    amax = np.abs(w).max(1)
    if fmt == "e4m3":
        byte = np.frexp(amax)[1] - 1 + 127 - 7
    else:
        mant, ex = np.frexp(amax / 6.0)
        byte = np.where(mant > 0.5, ex, ex - 1) + 127
    byte = np.clip(np.where(amax > 0, byte, 1), 1, 254)
    scaled = (w * np.exp2(127.0 - byte)[:, None, :]).reshape(k, n).astype(np.float32)
    by_word = np.ascontiguousarray(scaled.reshape(k // 512, 128, 4, n).transpose(0, 1, 3, 2))
    if fmt == "e4m3":
        words = by_word.astype(ml_dtypes.float8_e4m3fn).view(np.uint8)
    else:
        c = by_word.astype(ml_dtypes.float4_e2m1fn).view(np.uint8) & 0xF
        words = c[..., 0::2] | (c[..., 1::2] << 4)
    return np.ascontiguousarray(words), np.ascontiguousarray(byte.astype(np.uint8).reshape(k // 512, 16, n))


def unpack_weight(words, scales, fmt):
    g, p, n, _ = words.shape
    if fmt == "e4m3":
        vals = np.ascontiguousarray(words).view(ml_dtypes.float8_e4m3fn).astype(np.float64)
    else:
        nib = np.empty((g, p, n, 4), np.uint8)
        nib[..., 0::2] = words & 0xF
        nib[..., 1::2] = words >> 4
        vals = E2M1[nib]
    vals = vals * np.repeat(np.exp2(scales.astype(np.float64) - 127.0), 8, axis=1)[..., None]
    return vals.transpose(0, 1, 3, 2).reshape(g * 512, n)

def pack4(w):
    words, scales = pack_weight(w, "e2m1")
    return words.reshape(words.shape[0], 128, -1), scales


def unpack4(words, scales):
    return unpack_weight(words.reshape(words.shape[0], 128, -1, 2), scales, "e2m1")


B, T, C, H, D, R = 1, 128, 16384, 16, 128, 512
EPS = 1e-6
THETA = 10000.0


def rmsnorm(v, w):
    var = np.mean(v * v, axis=-1, keepdims=True)
    return v * (1.0 / np.sqrt(var + EPS)) * w


def rope(v, cos, sin):
    re, im = v[..., 0::2], v[..., 1::2]
    c, s = cos[None, :, None, :], sin[None, :, None, :]
    return np.stack([re * c - im * s, re * s + im * c], axis=-1).reshape(v.shape)


def setup_inputs():
    s = mx_kscale(C)
    ang = np.outer(np.arange(T), 1.0 / THETA ** (np.arange(0, D, 2) / D))
    x = bf(np.random.standard_normal((B, T, C)) * s)
    wq = np.random.standard_normal((H * D, C)) / np.sqrt(C) / s[None, :]
    wq_words, wq_scales = pack4(np.ascontiguousarray(wq.T))
    q_norm_w = bf(1.0 + 0.1 * np.random.standard_normal(D))
    return {"x": x,
            "wq_words": wq_words, "wq_scales": wq_scales,
            "q_norm_w": q_norm_w,
            "freqs_cos": bf(np.cos(ang)), "freqs_sin": bf(np.sin(ang))}


def reference(x, wq_words, wq_scales, q_norm_w, freqs_cos, freqs_sin):
    xq = (mxq(f64(x), 2, "e4m3") @ unpack4(wq_words, wq_scales)).reshape(B, T, H, D)
    return rope(rmsnorm(xq, f64(q_norm_w)), f64(freqs_cos), f64(freqs_sin))

@@ -1,0 +1,250 @@
+from contextlib import ExitStack
+
+import concourse.mybir as mybir
+from concourse.masks import make_identity
+
+F32 = mybir.dt.float32
+BF16 = mybir.dt.bfloat16
+I32 = mybir.dt.int32
+U32 = mybir.dt.uint32
+U8 = mybir.dt.uint8
+FP8X4 = mybir.dt.float8_e4m3fn_x4
+FP4X4 = mybir.dt.float4_e2m1fn_x4
+MULT = mybir.AluOpType.mult
+ADD = mybir.AluOpType.add
+ACT = mybir.ActivationFunctionType
+
+P = 128
+C = 16384
+HEADS = 16
+D = 128
+PAIRS = D // 2
+N = HEADS * D
+EPS = 1e-6
+
+K_PASS = 512
+GROUPS = C // K_PASS
+BANK = 512
+BANKS = N // BANK
+BANK_HEADS = BANK // D
+WORD_BYTES = 2
+
+CHUNK = 8
+CHUNKS = GROUPS // CHUNK
+PLANE_GROUPS = 8
+LOAD_GROUPS = 2
+TAIL = 10
+TAIL_LOAD_GROUPS = 5
+LOADS = (GROUPS - TAIL) // LOAD_GROUPS
+RING = 8
+
+FLOPS = 2 * P * C * N
+
+
+def tile_mla_pb_k_kernel(tc, x, wq_words, wq_scales, q_norm_w, freqs_cos, freqs_sin, out):
+    nc = tc.nc
+    x_rows = x.rearrange("o t c -> (o t) c")
+    out_rows = out.rearrange("o t h d -> (o t) (h d)")
+    words_i32 = wq_words.bitcast(I32)
+    scales_i32 = wq_scales.bitcast(I32)
+
+    with ExitStack() as ctx:
+        ctx.enter_context(tc.manual_schedule())
+        keep = ctx.enter_context(tc.tile_pool(name="keep", bufs=1))
+        w_pool = ctx.enter_context(tc.tile_pool(name="w_pool", bufs=RING))
+        end_pool = ctx.enter_context(tc.tile_pool(name="end_pool", bufs=2))
+        acc_pool = ctx.enter_context(tc.psum_pool(name="acc_pool", bufs=1))
+        turn_pool = ctx.enter_context(tc.psum_pool(name="turn_pool", bufs=BANKS))
+
+        eps = keep.tile([P, 1], F32)
+        nc.vector.memset(eps[:], EPS)
+        planes = [
+            keep.tile([P, PLANE_GROUPS, N], U8, name="planes%d" % i, align_bytes=64)
+            for i in range(GROUPS // PLANE_GROUPS)
+        ]
+        for plane in planes:
+            nc.vector.memset(plane[:].bitcast(I32), 0)
+        x_codes = keep.tile([P, GROUPS * P], U32, align_bytes=64)
+        x_scales = keep.tile([P, GROUPS * P], U8, align_bytes=64)
+        acc = [acc_pool.tile([P, BANK], F32, name="acc%d" % b) for b in range(BANKS)]
+
+        identity = keep.tile([P, P], F32)
+        make_identity(nc, identity[:])
+        ones = keep.tile([P, P], BF16)
+        nc.gpsimd.memset(ones[:], 1.0)
+        gain_row = keep.tile([P, D], BF16)
+        nc.gpsimd.memset(gain_row[:], 0.0)
+
+        cos = keep.tile([P, PAIRS], BF16)
+        sin = keep.tile([P, PAIRS], BF16)
+        nc.scalar.dma_start(out=gain_row[0:1, :], in_=q_norm_w.rearrange("(o d) -> o d", o=1))
+        nc.scalar.dma_start(out=cos[:], in_=freqs_cos)
+        nc.scalar.dma_start(out=sin[:], in_=freqs_sin)
+        warm = keep.tile([P, 1], F32)
+        nc.scalar.activation(out=warm[:], in_=eps[:], func=ACT.Sqrt)
+
+        w_words = {}
+
+        def load_words(i):
+            g0 = i * LOAD_GROUPS
+            w_pair = w_pool.tile([P, LOAD_GROUPS, WORD_BYTES * N], U8, align_bytes=64)
+            nc.sync.dma_start(
+                out=w_pair[:].bitcast(I32),
+                in_=words_i32[g0 : g0 + LOAD_GROUPS].rearrange("g p c -> p g c"),
+            )
+            for j in range(LOAD_GROUPS):
+                for b in range(BANKS):
+                    w_words[(g0 + j, b)] = w_pair[
+                        :, j, WORD_BYTES * BANK * b : WORD_BYTES * BANK * (b + 1)
+                    ]
+
+        with tc.tile_pool(name="x_pool", bufs=CHUNKS) as x_pool, tc.tile_pool(
+            name="grouped_pool", bufs=2
+        ) as grouped_pool:
+            x_raw = []
+            for c in range(CHUNKS):
+                x_chunk = x_pool.tile([P, CHUNK * K_PASS], BF16)
+                cols = slice(c * CHUNK * K_PASS, (c + 1) * CHUNK * K_PASS)
+                nc.sync.dma_start(out=x_chunk[:], in_=x_rows[:, cols])
+                x_raw.append(x_chunk)
+            for i in range(GROUPS // PLANE_GROUPS):
+                plane_i32 = planes[i][:].bitcast(I32)
+                for half in range(2):
+                    for r in range(4):
+                        nc.sync.dma_start(
+                            out=plane_i32[32 * half + r : P : 64, :, :],
+                            in_=scales_i32[
+                                i * PLANE_GROUPS : (i + 1) * PLANE_GROUPS, 4 * half + r : 16 : 8, :
+                            ].rearrange("g q n -> q g n"),
+                        )
+            for i in range(RING):
+                load_words(i)
+
+            def quantise(c, grouped):
+                cols = slice(c * CHUNK * P, (c + 1) * CHUNK * P)
+                nc.vector.quantize_mx(
+                    out=x_codes[:, cols].bitcast(FP8X4), scales=x_scales[:, cols], in_=grouped[:]
+                )
+
+            waiting = None
+            for c in range(CHUNKS):
+                x_f32 = x_raw[c][:].bitcast(F32)
+                grouped = grouped_pool.tile([P, CHUNK * K_PASS], BF16, align_bytes=64)
+                grouped_f32 = grouped[:].bitcast(F32).rearrange("p (g m u) -> p g m u", g=CHUNK, u=2)
+                for i in range(CHUNK // 2):
+                    turned = turn_pool.tile([P, 2, 2, P], F32, tag="turn")
+                    for j in range(2):
+                        w0 = (2 * i + j) * (K_PASS // 2)
+                        for u in range(2):
+                            nc.tensor.transpose(
+                                turned[:, j, u, :], x_f32[:, w0 + u : w0 + K_PASS // 2 : 2], identity[:]
+                            )
+                    source = turned[:].rearrange("p g u m -> p g m u")
+                    if i % 2 == 0:
+                        nc.vector.tensor_copy(out=grouped_f32[:, 2 * i : 2 * i + 2], in_=source)
+                    else:
+                        nc.scalar.copy(out=grouped_f32[:, 2 * i : 2 * i + 2], in_=source)
+                if waiting is not None:
+                    quantise(c - 1, waiting)
+                waiting = grouped
+            quantise(CHUNKS - 1, waiting)
+
+        gain_bank = turn_pool.tile([P, BANK], F32, tag="turn")
+        nc.tensor.matmul(out=gain_bank[:, 0:D], lhsT=ones[:], rhs=gain_row[:], start=True, stop=True)
+        gain = gain_bank[:, 0:D].rearrange("p (j e) -> p j e", e=2)
+        tab_cos = keep.tile([P, D], F32)
+        tab_sin = keep.tile([P, 2, PAIRS], F32)
+        nc.vector.tensor_tensor(
+            out=tab_cos[:].rearrange("p (j e) -> p j e", e=2),
+            in0=gain,
+            in1=cos[:].unsqueeze(2).to_broadcast([P, PAIRS, 2]),
+            op=MULT,
+        )
+        nc.vector.scalar_tensor_tensor(
+            out=tab_sin[:, 0, :], in0=gain[:, :, 1], scalar=-1.0, in1=sin[:], op0=MULT, op1=MULT
+        )
+        nc.vector.tensor_tensor(out=tab_sin[:, 1, :], in0=gain[:, :, 0], in1=sin[:], op=MULT)
+
+        def mx_pass(g, b):
+            nc.tensor.matmul_mx(
+                out=acc[b][:],
+                lhsT=x_codes[:, g * P : (g + 1) * P].bitcast(FP8X4),
+                lhsT_scale=x_scales[:, g * P : (g + 1) * P],
+                rhs=w_words[(g, b)].bitcast(FP4X4),
+                rhs_scale=planes[g // PLANE_GROUPS][:, g % PLANE_GROUPS, BANK * b : BANK * (b + 1)],
+                start=(g == 0),
+                stop=(g == GROUPS - 1),
+            )
+
+        for i in range(LOADS):
+            for g in range(i * LOAD_GROUPS, (i + 1) * LOAD_GROUPS):
+                for b in range(BANKS):
+                    mx_pass(g, b)
+            if i + RING < LOADS:
+                load_words(i + RING)
+
+        tail_pool = ctx.enter_context(
+            tc.tile_pool(name="tail_pool", bufs=BANKS * TAIL // TAIL_LOAD_GROUPS)
+        )
+        for b in range(BANKS):
+            cols = slice(BANK * b // 2, BANK * (b + 1) // 2)
+            for g0 in range(GROUPS - TAIL, GROUPS, TAIL_LOAD_GROUPS):
+                w_part = tail_pool.tile([P, TAIL_LOAD_GROUPS, WORD_BYTES * BANK], U8, align_bytes=64)
+                nc.sync.dma_start(
+                    out=w_part[:].bitcast(I32),
+                    in_=words_i32[g0 : g0 + TAIL_LOAD_GROUPS, :, cols].rearrange("g p c -> p g c"),
+                )
+                for j in range(TAIL_LOAD_GROUPS):
+                    w_words[(g0 + j, b)] = w_part[:, j, :]
+
+        for b in range(BANKS):
+            for g in range(GROUPS - TAIL, GROUPS):
+                mx_pass(g, b)
+
+            q_sb = end_pool.tile([P, BANK], F32)
+            nc.scalar.copy(out=q_sb[:], in_=acc[b][:])
+            squares = end_pool.tile([P, BANK], F32)
+            sums = end_pool.tile([P, BANK_HEADS], F32)
+            for h in range(BANK_HEADS):
+                nc.scalar.activation(
+                    out=squares[:, h * D : (h + 1) * D],
+                    in_=acc[b][:, h * D : (h + 1) * D],
+                    func=ACT.Square,
+                    accum_out=sums[:, h : h + 1],
+                )
+            rms = end_pool.tile([P, BANK_HEADS], F32)
+            nc.scalar.activation(out=rms[:], in_=sums[:], func=ACT.Sqrt, scale=1.0 / D, bias=eps[:])
+
+            q_pairs = q_sb[:].rearrange("p (h j e) -> p h j e", h=BANK_HEADS, e=2)
+            straight = end_pool.tile([P, BANK], F32)
+            nc.vector.tensor_tensor(
+                out=straight[:].rearrange("p (h d) -> p h d", h=BANK_HEADS),
+                in0=q_sb[:].rearrange("p (h d) -> p h d", h=BANK_HEADS),
+                in1=tab_cos[:].unsqueeze(1).to_broadcast([P, BANK_HEADS, D]),
+                op=MULT,
+            )
+            crossed = end_pool.tile([P, 2, BANK // 2], F32)
+            for e in range(2):
+                nc.vector.tensor_tensor(
+                    out=crossed[:, e, :].rearrange("p (h j) -> p h j", h=BANK_HEADS),
+                    in0=q_pairs[:, :, :, 1 - e],
+                    in1=tab_sin[:, e, :].unsqueeze(1).to_broadcast([P, BANK_HEADS, PAIRS]),
+                    op=MULT,
+                )
+            rotated = end_pool.tile([P, BANK], F32)
+            nc.vector.tensor_tensor(
+                out=rotated[:].rearrange("p (n e) -> p n e", e=2),
+                in0=straight[:].rearrange("p (n e) -> p n e", e=2),
+                in1=crossed[:].rearrange("p e n -> p n e"),
+                op=ADD,
+            )
+            rstd = end_pool.tile([P, BANK_HEADS], F32)
+            nc.vector.reciprocal(out=rstd[:], in_=rms[:])
+            result = end_pool.tile([P, BANK], F32)
+            nc.vector.tensor_tensor(
+                out=result[:].rearrange("p (h d) -> p h d", h=BANK_HEADS),
+                in0=rotated[:].rearrange("p (h d) -> p h d", h=BANK_HEADS),
+                in1=rstd[:].unsqueeze(2).to_broadcast([P, BANK_HEADS, D]),
+                op=MULT,
+            )
+            nc.sync.dma_start(out=out_rows[:, BANK * b : BANK * (b + 1)], in_=result[:])

@@ -107,6 +107,8 @@ def tile_mla_pb_k_kernel(tc, x, wq_words, wq_scales, q_norm_w, freqs_cos, freqs_
                 cols = slice(c * CHUNK * K_PASS, (c + 1) * CHUNK * K_PASS)
                 nc.sync.dma_start(out=x_chunk[:], in_=x_rows[:, cols])
                 x_raw.append(x_chunk)
+            for i in range(RING):
+                load_words(i)
             for i in range(GROUPS // PLANE_GROUPS):
                 plane_i32 = planes[i][:].bitcast(I32)
                 for half in range(2):
@@ -117,8 +119,6 @@ def tile_mla_pb_k_kernel(tc, x, wq_words, wq_scales, q_norm_w, freqs_cos, freqs_
                                 i * PLANE_GROUPS : (i + 1) * PLANE_GROUPS, 4 * half + r : 16 : 8, :
                             ].rearrange("g q n -> q g n"),
                         )
-            for i in range(RING):
-                load_words(i)
 
             def quantise(c, grouped):
                 cols = slice(c * CHUNK * P, (c + 1) * CHUNK * P)

@@ -33,9 +33,11 @@ CHUNK = 8
 CHUNKS = GROUPS // CHUNK
 PLANE_GROUPS = 8
 LOAD_GROUPS = 2
-TAIL = 10
-TAIL_LOAD_GROUPS = 5
+TAIL_PARTS = (4, 2)
+TAIL = sum(TAIL_PARTS)
 LOADS = (GROUPS - TAIL) // LOAD_GROUPS
+VECTOR_HEADS = 2
+FIRST_LOADS = 6
 RING = 8
 
 FLOPS = 2 * P * C * N
@@ -107,7 +109,7 @@ def tile_mla_pb_k_kernel(tc, x, wq_words, wq_scales, q_norm_w, freqs_cos, freqs_
                 cols = slice(c * CHUNK * K_PASS, (c + 1) * CHUNK * K_PASS)
                 nc.sync.dma_start(out=x_chunk[:], in_=x_rows[:, cols])
                 x_raw.append(x_chunk)
-            for i in range(RING):
+            for i in range(FIRST_LOADS):
                 load_words(i)
             for i in range(GROUPS // PLANE_GROUPS):
                 plane_i32 = planes[i][:].bitcast(I32)
@@ -119,6 +121,8 @@ def tile_mla_pb_k_kernel(tc, x, wq_words, wq_scales, q_norm_w, freqs_cos, freqs_
                                 i * PLANE_GROUPS : (i + 1) * PLANE_GROUPS, 4 * half + r : 16 : 8, :
                             ].rearrange("g q n -> q g n"),
                         )
+            for i in range(FIRST_LOADS, RING):
+                load_words(i)
 
             def quantise(c, grouped):
                 cols = slice(c * CHUNK * P, (c + 1) * CHUNK * P)
@@ -152,18 +156,18 @@ def tile_mla_pb_k_kernel(tc, x, wq_words, wq_scales, q_norm_w, freqs_cos, freqs_
         gain_bank = turn_pool.tile([P, BANK], F32, tag="turn")
         nc.tensor.matmul(out=gain_bank[:, 0:D], lhsT=ones[:], rhs=gain_row[:], start=True, stop=True)
         gain = gain_bank[:, 0:D].rearrange("p (j e) -> p j e", e=2)
-        tab_cos = keep.tile([P, D], F32)
-        tab_sin = keep.tile([P, 2, PAIRS], F32)
+        tab = keep.tile([P, 2, D], F32)
+        to_other = tab[:, 1, :].rearrange("p (j e) -> p j e", e=2)
         nc.vector.tensor_tensor(
-            out=tab_cos[:].rearrange("p (j e) -> p j e", e=2),
+            out=tab[:, 0, :].rearrange("p (j e) -> p j e", e=2),
             in0=gain,
             in1=cos[:].unsqueeze(2).to_broadcast([P, PAIRS, 2]),
             op=MULT,
         )
+        nc.vector.tensor_tensor(out=to_other[:, :, 0], in0=gain[:, :, 0], in1=sin[:], op=MULT)
         nc.vector.scalar_tensor_tensor(
-            out=tab_sin[:, 0, :], in0=gain[:, :, 1], scalar=-1.0, in1=sin[:], op0=MULT, op1=MULT
+            out=to_other[:, :, 1], in0=gain[:, :, 1], scalar=-1.0, in1=sin[:], op0=MULT, op1=MULT
         )
-        nc.vector.tensor_tensor(out=tab_sin[:, 1, :], in0=gain[:, :, 0], in1=sin[:], op=MULT)
 
         def mx_pass(g, b):
             nc.tensor.matmul_mx(
@@ -183,26 +187,21 @@ def tile_mla_pb_k_kernel(tc, x, wq_words, wq_scales, q_norm_w, freqs_cos, freqs_
             if i + RING < LOADS:
                 load_words(i + RING)
 
-        tail_pool = ctx.enter_context(
-            tc.tile_pool(name="tail_pool", bufs=BANKS * TAIL // TAIL_LOAD_GROUPS)
-        )
+        tail_pool = ctx.enter_context(tc.tile_pool(name="tail_pool", bufs=BANKS))
         for b in range(BANKS):
             cols = slice(BANK * b // 2, BANK * (b + 1) // 2)
-            for g0 in range(GROUPS - TAIL, GROUPS, TAIL_LOAD_GROUPS):
-                w_part = tail_pool.tile([P, TAIL_LOAD_GROUPS, WORD_BYTES * BANK], U8, align_bytes=64)
+            g0 = GROUPS - TAIL
+            for i, n in enumerate(TAIL_PARTS):
+                w_part = tail_pool.tile([P, n, WORD_BYTES * BANK], U8, name="w_part%d" % i, align_bytes=64)
                 nc.sync.dma_start(
                     out=w_part[:].bitcast(I32),
-                    in_=words_i32[g0 : g0 + TAIL_LOAD_GROUPS, :, cols].rearrange("g p c -> p g c"),
+                    in_=words_i32[g0 : g0 + n, :, cols].rearrange("g p c -> p g c"),
                 )
-                for j in range(TAIL_LOAD_GROUPS):
+                for j in range(n):
                     w_words[(g0 + j, b)] = w_part[:, j, :]
+                g0 += n
 
-        for b in range(BANKS):
-            for g in range(GROUPS - TAIL, GROUPS):
-                mx_pass(g, b)
-
-            q_sb = end_pool.tile([P, BANK], F32)
-            nc.scalar.copy(out=q_sb[:], in_=acc[b][:])
+        def root_mean_squares(b):
             squares = end_pool.tile([P, BANK], F32)
             sums = end_pool.tile([P, BANK_HEADS], F32)
             for h in range(BANK_HEADS):
@@ -214,37 +213,56 @@ def tile_mla_pb_k_kernel(tc, x, wq_words, wq_scales, q_norm_w, freqs_cos, freqs_
                 )
             rms = end_pool.tile([P, BANK_HEADS], F32)
             nc.scalar.activation(out=rms[:], in_=sums[:], func=ACT.Sqrt, scale=1.0 / D, bias=eps[:])
+            return rms
 
-            q_pairs = q_sb[:].rearrange("p (h j e) -> p h j e", h=BANK_HEADS, e=2)
-            straight = end_pool.tile([P, BANK], F32)
+        def rotate(b):
+            products = end_pool.tile([P, 2, BANK], F32)
             nc.vector.tensor_tensor(
-                out=straight[:].rearrange("p (h d) -> p h d", h=BANK_HEADS),
-                in0=q_sb[:].rearrange("p (h d) -> p h d", h=BANK_HEADS),
-                in1=tab_cos[:].unsqueeze(1).to_broadcast([P, BANK_HEADS, D]),
+                out=products[:].rearrange("p s (h d) -> p s h d", h=BANK_HEADS),
+                in0=acc[b][:]
+                .rearrange("p (h d) -> p h d", h=BANK_HEADS)
+                .unsqueeze(1)
+                .to_broadcast([P, 2, BANK_HEADS, D]),
+                in1=tab[:].unsqueeze(2).to_broadcast([P, 2, BANK_HEADS, D]),
                 op=MULT,
             )
-            crossed = end_pool.tile([P, 2, BANK // 2], F32)
-            for e in range(2):
-                nc.vector.tensor_tensor(
-                    out=crossed[:, e, :].rearrange("p (h j) -> p h j", h=BANK_HEADS),
-                    in0=q_pairs[:, :, :, 1 - e],
-                    in1=tab_sin[:, e, :].unsqueeze(1).to_broadcast([P, BANK_HEADS, PAIRS]),
-                    op=MULT,
-                )
             rotated = end_pool.tile([P, BANK], F32)
             nc.vector.tensor_tensor(
                 out=rotated[:].rearrange("p (n e) -> p n e", e=2),
-                in0=straight[:].rearrange("p (n e) -> p n e", e=2),
-                in1=crossed[:].rearrange("p e n -> p n e"),
+                in0=products[:, 0, :].rearrange("p (n e) -> p n e", e=2),
+                in1=products[:, 1, :].rearrange("p (n e) -> p n e", e=2)[:, :, ::-1],
                 op=ADD,
             )
+            return rotated
+
+        def divide_and_store(b, rotated, rstd, vector_heads):
+            result = end_pool.tile([P, BANK], F32)
+            if vector_heads > 0:
+                split = vector_heads * D
+                nc.vector.tensor_tensor(
+                    out=result[:, 0:split].rearrange("p (h d) -> p h d", h=vector_heads),
+                    in0=rotated[:, 0:split].rearrange("p (h d) -> p h d", h=vector_heads),
+                    in1=rstd[:, 0:vector_heads].unsqueeze(2).to_broadcast([P, vector_heads, D]),
+                    op=MULT,
+                )
+            for h in range(vector_heads, BANK_HEADS):
+                nc.scalar.activation(
+                    out=result[:, h * D : (h + 1) * D],
+                    in_=rotated[:, h * D : (h + 1) * D],
+                    func=ACT.Copy,
+                    scale=rstd[:, h : h + 1],
+                )
+            nc.sync.dma_start(out=out_rows[:, BANK * b : BANK * (b + 1)], in_=result[:])
+
+        waiting = None
+        for b in range(BANKS):
+            for g in range(GROUPS - TAIL, GROUPS):
+                mx_pass(g, b)
+            rms = root_mean_squares(b)
+            if waiting is not None:
+                divide_and_store(*waiting, 0)
+            rotated = rotate(b)
             rstd = end_pool.tile([P, BANK_HEADS], F32)
             nc.vector.reciprocal(out=rstd[:], in_=rms[:])
-            result = end_pool.tile([P, BANK], F32)
-            nc.vector.tensor_tensor(
-                out=result[:].rearrange("p (h d) -> p h d", h=BANK_HEADS),
-                in0=rotated[:].rearrange("p (h d) -> p h d", h=BANK_HEADS),
-                in1=rstd[:].unsqueeze(2).to_broadcast([P, BANK_HEADS, D]),
-                op=MULT,
-            )
-            nc.sync.dma_start(out=out_rows[:, BANK * b : BANK * (b + 1)], in_=result[:])
+            waiting = (b, rotated, rstd)
+        divide_and_store(*waiting, VECTOR_HEADS)

@@ -32,6 +32,7 @@ WORD_BYTES = 2
 CHUNK = 8
 CHUNKS = GROUPS // CHUNK
 PLANE_GROUPS = 8
+SCALE_LOADS = ((0, 8), (8, 8), (16, 8), (24, 4), (28, 4))
 LOAD_GROUPS = 2
 TAIL_PARTS = (4, 2)
 TAIL = sum(TAIL_PARTS)
@@ -111,15 +112,14 @@ def tile_mla_pb_k_kernel(tc, x, wq_words, wq_scales, q_norm_w, freqs_cos, freqs_
                 x_raw.append(x_chunk)
             for i in range(FIRST_LOADS):
                 load_words(i)
-            for i in range(GROUPS // PLANE_GROUPS):
-                plane_i32 = planes[i][:].bitcast(I32)
+            for g0, n in SCALE_LOADS:
+                plane_i32 = planes[g0 // PLANE_GROUPS][:].bitcast(I32)
+                at = g0 % PLANE_GROUPS
                 for half in range(2):
                     for r in range(4):
                         nc.sync.dma_start(
-                            out=plane_i32[32 * half + r : P : 64, :, :],
-                            in_=scales_i32[
-                                i * PLANE_GROUPS : (i + 1) * PLANE_GROUPS, 4 * half + r : 16 : 8, :
-                            ].rearrange("g q n -> q g n"),
+                            out=plane_i32[32 * half + r : P : 64, at : at + n, :],
+                            in_=scales_i32[g0 : g0 + n, 4 * half + r : 16 : 8, :].rearrange("g q n -> q g n"),
                         )
             for i in range(FIRST_LOADS, RING):
                 load_words(i)

@@ -34,7 +34,7 @@ CHUNKS = GROUPS // CHUNK
 PLANE_GROUPS = 8
 SCALE_LOADS = ((0, 8), (8, 8), (16, 8), (24, 4), (28, 4))
 LOAD_GROUPS = 2
-TAIL_PARTS = (4, 2)
+TAIL_PARTS = (4, 2, 1, 1)
 TAIL = sum(TAIL_PARTS)
 LOADS = (GROUPS - TAIL) // LOAD_GROUPS
 VECTOR_HEADS = 2
@@ -215,12 +215,11 @@ def tile_mla_pb_k_kernel(tc, x, wq_words, wq_scales, q_norm_w, freqs_cos, freqs_
             nc.scalar.activation(out=rms[:], in_=sums[:], func=ACT.Sqrt, scale=1.0 / D, bias=eps[:])
             return rms
 
-        def rotate(b):
+        def rotate(q):
             products = end_pool.tile([P, 2, BANK], F32)
             nc.vector.tensor_tensor(
                 out=products[:].rearrange("p s (h d) -> p s h d", h=BANK_HEADS),
-                in0=acc[b][:]
-                .rearrange("p (h d) -> p h d", h=BANK_HEADS)
+                in0=q.rearrange("p (h d) -> p h d", h=BANK_HEADS)
                 .unsqueeze(1)
                 .to_broadcast([P, 2, BANK_HEADS, D]),
                 in1=tab[:].unsqueeze(2).to_broadcast([P, 2, BANK_HEADS, D]),
@@ -258,10 +257,15 @@ def tile_mla_pb_k_kernel(tc, x, wq_words, wq_scales, q_norm_w, freqs_cos, freqs_
         for b in range(BANKS):
             for g in range(GROUPS - TAIL, GROUPS):
                 mx_pass(g, b)
+            q = acc[b][:]
+            if b == BANKS - 1:
+                q_sb = end_pool.tile([P, BANK], F32)
+                nc.scalar.copy(out=q_sb[:], in_=q)
+                q = q_sb[:]
             rms = root_mean_squares(b)
             if waiting is not None:
                 divide_and_store(*waiting, 0)
-            rotated = rotate(b)
+            rotated = rotate(q)
             rstd = end_pool.tile([P, BANK_HEADS], F32)
             nc.vector.reciprocal(out=rstd[:], in_=rms[:])
             waiting = (b, rotated, rstd)

from contextlib import ExitStack

import concourse.mybir as mybir
from concourse.masks import make_identity

F32 = mybir.dt.float32
BF16 = mybir.dt.bfloat16
I32 = mybir.dt.int32
U32 = mybir.dt.uint32
U8 = mybir.dt.uint8
FP8X4 = mybir.dt.float8_e4m3fn_x4
FP4X4 = mybir.dt.float4_e2m1fn_x4
MULT = mybir.AluOpType.mult
ADD = mybir.AluOpType.add
ACT = mybir.ActivationFunctionType

P = 128
C = 16384
HEADS = 16
D = 128
PAIRS = D // 2
N = HEADS * D
EPS = 1e-6

K_PASS = 512
GROUPS = C // K_PASS
BANK = 512
BANKS = N // BANK
BANK_HEADS = BANK // D
WORD_BYTES = 2

CHUNK = 8
CHUNKS = GROUPS // CHUNK
PLANE_GROUPS = 8
SCALE_LOADS = ((0, 8), (8, 8), (16, 8), (24, 4), (28, 4))
LOAD_GROUPS = 2
TAIL_PARTS = (4, 2, 1, 1)
TAIL = sum(TAIL_PARTS)
LOADS = (GROUPS - TAIL) // LOAD_GROUPS
VECTOR_HEADS = 2
FIRST_LOADS = 6
RING = 8

FLOPS = 2 * P * C * N


def tile_mla_pb_k_kernel(tc, x, wq_words, wq_scales, q_norm_w, freqs_cos, freqs_sin, out):
    nc = tc.nc
    x_rows = x.rearrange("o t c -> (o t) c")
    out_rows = out.rearrange("o t h d -> (o t) (h d)")
    words_i32 = wq_words.bitcast(I32)
    scales_i32 = wq_scales.bitcast(I32)

    with ExitStack() as ctx:
        ctx.enter_context(tc.manual_schedule())
        keep = ctx.enter_context(tc.tile_pool(name="keep", bufs=1))
        w_pool = ctx.enter_context(tc.tile_pool(name="w_pool", bufs=RING))
        end_pool = ctx.enter_context(tc.tile_pool(name="end_pool", bufs=2))
        acc_pool = ctx.enter_context(tc.psum_pool(name="acc_pool", bufs=1))
        turn_pool = ctx.enter_context(tc.psum_pool(name="turn_pool", bufs=BANKS))

        eps = keep.tile([P, 1], F32)
        nc.vector.memset(eps[:], EPS)
        planes = [
            keep.tile([P, PLANE_GROUPS, N], U8, name="planes%d" % i, align_bytes=64)
            for i in range(GROUPS // PLANE_GROUPS)
        ]
        for plane in planes:
            nc.vector.memset(plane[:].bitcast(I32), 0)
        x_codes = keep.tile([P, GROUPS * P], U32, align_bytes=64)
        x_scales = keep.tile([P, GROUPS * P], U8, align_bytes=64)
        acc = [acc_pool.tile([P, BANK], F32, name="acc%d" % b) for b in range(BANKS)]

        identity = keep.tile([P, P], F32)
        make_identity(nc, identity[:])
        ones = keep.tile([P, P], BF16)
        nc.gpsimd.memset(ones[:], 1.0)
        gain_row = keep.tile([P, D], BF16)
        nc.gpsimd.memset(gain_row[:], 0.0)

        cos = keep.tile([P, PAIRS], BF16)
        sin = keep.tile([P, PAIRS], BF16)
        nc.scalar.dma_start(out=gain_row[0:1, :], in_=q_norm_w.rearrange("(o d) -> o d", o=1))
        nc.scalar.dma_start(out=cos[:], in_=freqs_cos)
        nc.scalar.dma_start(out=sin[:], in_=freqs_sin)
        warm = keep.tile([P, 1], F32)
        nc.scalar.activation(out=warm[:], in_=eps[:], func=ACT.Sqrt)

        w_words = {}

        def load_words(i):
            g0 = i * LOAD_GROUPS
            w_pair = w_pool.tile([P, LOAD_GROUPS, WORD_BYTES * N], U8, align_bytes=64)
            nc.sync.dma_start(
                out=w_pair[:].bitcast(I32),
                in_=words_i32[g0 : g0 + LOAD_GROUPS].rearrange("g p c -> p g c"),
            )
            for j in range(LOAD_GROUPS):
                for b in range(BANKS):
                    w_words[(g0 + j, b)] = w_pair[
                        :, j, WORD_BYTES * BANK * b : WORD_BYTES * BANK * (b + 1)
                    ]

        with tc.tile_pool(name="x_pool", bufs=CHUNKS) as x_pool, tc.tile_pool(
            name="grouped_pool", bufs=2
        ) as grouped_pool:
            x_raw = []
            for c in range(CHUNKS):
                x_chunk = x_pool.tile([P, CHUNK * K_PASS], BF16)
                cols = slice(c * CHUNK * K_PASS, (c + 1) * CHUNK * K_PASS)
                nc.sync.dma_start(out=x_chunk[:], in_=x_rows[:, cols])
                x_raw.append(x_chunk)
            for i in range(FIRST_LOADS):
                load_words(i)
            for g0, n in SCALE_LOADS:
                plane_i32 = planes[g0 // PLANE_GROUPS][:].bitcast(I32)
                at = g0 % PLANE_GROUPS
                for half in range(2):
                    for r in range(4):
                        nc.sync.dma_start(
                            out=plane_i32[32 * half + r : P : 64, at : at + n, :],
                            in_=scales_i32[g0 : g0 + n, 4 * half + r : 16 : 8, :].rearrange("g q n -> q g n"),
                        )
            for i in range(FIRST_LOADS, RING):
                load_words(i)

            def quantise(c, grouped):
                cols = slice(c * CHUNK * P, (c + 1) * CHUNK * P)
                nc.vector.quantize_mx(
                    out=x_codes[:, cols].bitcast(FP8X4), scales=x_scales[:, cols], in_=grouped[:]
                )

            waiting = None
            for c in range(CHUNKS):
                x_f32 = x_raw[c][:].bitcast(F32)
                grouped = grouped_pool.tile([P, CHUNK * K_PASS], BF16, align_bytes=64)
                grouped_f32 = grouped[:].bitcast(F32).rearrange("p (g m u) -> p g m u", g=CHUNK, u=2)
                for i in range(CHUNK // 2):
                    turned = turn_pool.tile([P, 2, 2, P], F32, tag="turn")
                    for j in range(2):
                        w0 = (2 * i + j) * (K_PASS // 2)
                        for u in range(2):
                            nc.tensor.transpose(
                                turned[:, j, u, :], x_f32[:, w0 + u : w0 + K_PASS // 2 : 2], identity[:]
                            )
                    source = turned[:].rearrange("p g u m -> p g m u")
                    if i % 2 == 0:
                        nc.vector.tensor_copy(out=grouped_f32[:, 2 * i : 2 * i + 2], in_=source)
                    else:
                        nc.scalar.copy(out=grouped_f32[:, 2 * i : 2 * i + 2], in_=source)
                if waiting is not None:
                    quantise(c - 1, waiting)
                waiting = grouped
            quantise(CHUNKS - 1, waiting)

        gain_bank = turn_pool.tile([P, BANK], F32, tag="turn")
        nc.tensor.matmul(out=gain_bank[:, 0:D], lhsT=ones[:], rhs=gain_row[:], start=True, stop=True)
        gain = gain_bank[:, 0:D].rearrange("p (j e) -> p j e", e=2)
        tab = keep.tile([P, 2, D], F32)
        to_other = tab[:, 1, :].rearrange("p (j e) -> p j e", e=2)
        nc.vector.tensor_tensor(
            out=tab[:, 0, :].rearrange("p (j e) -> p j e", e=2),
            in0=gain,
            in1=cos[:].unsqueeze(2).to_broadcast([P, PAIRS, 2]),
            op=MULT,
        )
        nc.vector.tensor_tensor(out=to_other[:, :, 0], in0=gain[:, :, 0], in1=sin[:], op=MULT)
        nc.vector.scalar_tensor_tensor(
            out=to_other[:, :, 1], in0=gain[:, :, 1], scalar=-1.0, in1=sin[:], op0=MULT, op1=MULT
        )

        def mx_pass(g, b):
            nc.tensor.matmul_mx(
                out=acc[b][:],
                lhsT=x_codes[:, g * P : (g + 1) * P].bitcast(FP8X4),
                lhsT_scale=x_scales[:, g * P : (g + 1) * P],
                rhs=w_words[(g, b)].bitcast(FP4X4),
                rhs_scale=planes[g // PLANE_GROUPS][:, g % PLANE_GROUPS, BANK * b : BANK * (b + 1)],
                start=(g == 0),
                stop=(g == GROUPS - 1),
            )

        for i in range(LOADS):
            for g in range(i * LOAD_GROUPS, (i + 1) * LOAD_GROUPS):
                for b in range(BANKS):
                    mx_pass(g, b)
            if i + RING < LOADS:
                load_words(i + RING)

        tail_pool = ctx.enter_context(tc.tile_pool(name="tail_pool", bufs=BANKS))
        for b in range(BANKS):
            cols = slice(BANK * b // 2, BANK * (b + 1) // 2)
            g0 = GROUPS - TAIL
            for i, n in enumerate(TAIL_PARTS):
                w_part = tail_pool.tile([P, n, WORD_BYTES * BANK], U8, name="w_part%d" % i, align_bytes=64)
                nc.sync.dma_start(
                    out=w_part[:].bitcast(I32),
                    in_=words_i32[g0 : g0 + n, :, cols].rearrange("g p c -> p g c"),
                )
                for j in range(n):
                    w_words[(g0 + j, b)] = w_part[:, j, :]
                g0 += n

        def root_mean_squares(b):
            squares = end_pool.tile([P, BANK], F32)
            sums = end_pool.tile([P, BANK_HEADS], F32)
            for h in range(BANK_HEADS):
                nc.scalar.activation(
                    out=squares[:, h * D : (h + 1) * D],
                    in_=acc[b][:, h * D : (h + 1) * D],
                    func=ACT.Square,
                    accum_out=sums[:, h : h + 1],
                )
            rms = end_pool.tile([P, BANK_HEADS], F32)
            nc.scalar.activation(out=rms[:], in_=sums[:], func=ACT.Sqrt, scale=1.0 / D, bias=eps[:])
            return rms

        def rotate(q):
            products = end_pool.tile([P, 2, BANK], F32)
            nc.vector.tensor_tensor(
                out=products[:].rearrange("p s (h d) -> p s h d", h=BANK_HEADS),
                in0=q.rearrange("p (h d) -> p h d", h=BANK_HEADS)
                .unsqueeze(1)
                .to_broadcast([P, 2, BANK_HEADS, D]),
                in1=tab[:].unsqueeze(2).to_broadcast([P, 2, BANK_HEADS, D]),
                op=MULT,
            )
            rotated = end_pool.tile([P, BANK], F32)
            nc.vector.tensor_tensor(
                out=rotated[:].rearrange("p (n e) -> p n e", e=2),
                in0=products[:, 0, :].rearrange("p (n e) -> p n e", e=2),
                in1=products[:, 1, :].rearrange("p (n e) -> p n e", e=2)[:, :, ::-1],
                op=ADD,
            )
            return rotated

        def divide_and_store(b, rotated, rstd, vector_heads):
            result = end_pool.tile([P, BANK], F32)
            if vector_heads > 0:
                split = vector_heads * D
                nc.vector.tensor_tensor(
                    out=result[:, 0:split].rearrange("p (h d) -> p h d", h=vector_heads),
                    in0=rotated[:, 0:split].rearrange("p (h d) -> p h d", h=vector_heads),
                    in1=rstd[:, 0:vector_heads].unsqueeze(2).to_broadcast([P, vector_heads, D]),
                    op=MULT,
                )
            for h in range(vector_heads, BANK_HEADS):
                nc.scalar.activation(
                    out=result[:, h * D : (h + 1) * D],
                    in_=rotated[:, h * D : (h + 1) * D],
                    func=ACT.Copy,
                    scale=rstd[:, h : h + 1],
                )
            nc.sync.dma_start(out=out_rows[:, BANK * b : BANK * (b + 1)], in_=result[:])

        waiting = None
        for b in range(BANKS):
            for g in range(GROUPS - TAIL, GROUPS):
                mx_pass(g, b)
            q = acc[b][:]
            if b == BANKS - 1:
                q_sb = end_pool.tile([P, BANK], F32)
                nc.scalar.copy(out=q_sb[:], in_=q)
                q = q_sb[:]
            rms = root_mean_squares(b)
            if waiting is not None:
                divide_and_store(*waiting, 0)
            rotated = rotate(q)
            rstd = end_pool.tile([P, BANK_HEADS], F32)
            nc.vector.reciprocal(out=rstd[:], in_=rms[:])
            waiting = (b, rotated, rstd)
        divide_and_store(*waiting, VECTOR_HEADS)
